import numpy as np
import ml_dtypes

BF16 = ml_dtypes.bfloat16


def bf(x):
    return np.asarray(x, np.float32).astype(BF16)


def f32(x):
    return np.asarray(x, np.float32)


def f64(x):
    return np.asarray(x).astype(np.float64)


def striped(idx):
    return np.tile(idx.reshape(-1, 16).T, (8, 1))


NB, CH, S, K, C, N = 128, 8, 512, 4, 1024, 2048
TEMP = 0.5


def setup_inputs():
    return {"z": f32(np.random.standard_normal((C, S))), "ctx": f32(np.random.standard_normal((C, S))), "offs": striped(np.concatenate([np.random.permutation(S) for _ in range(K)]))}


def reference(z, ctx, offs):
    idx = offs[:16].T.reshape(-1)
    neg = f64(z)[:, idx].reshape(CH, NB, K, S)
    cc = f64(ctx).reshape(CH, NB, S)[:, :, None, :]
    dot = (neg * cc).sum(axis=0)
    tn = np.sqrt((neg * neg).sum(axis=0))
    cn = np.sqrt((cc * cc).sum(axis=0))
    return (dot / (cn * tn) / TEMP).reshape(NB, N)

@@ -1,0 +1,82 @@
+import concourse.mybir as mybir
+from concourse.masks import make_identity
+
+P = 128
+CH = 8
+S = 512
+K = 4
+TEMP = 0.5
+COLS = S // 16
+
+FLOPS = 2 * CH * P * K * S
+
+F32 = mybir.dt.float32
+U16 = mybir.dt.uint16
+MULT = mybir.AluOpType.mult
+SQUARE = mybir.ActivationFunctionType.Square
+RSQRT = mybir.ActivationFunctionType.Abs_reciprocal_sqrt
+
+
+def tile_contrastivessl_kernel(tc, z, ctx, offs, out):
+    nc = tc.nc
+    with (
+        tc.tile_pool(name="held", bufs=1) as held,
+        tc.tile_pool(name="squares", bufs=4) as squares,
+        tc.tile_pool(name="products", bufs=16) as products,
+        tc.tile_pool(name="results", bufs=2) as results,
+        tc.psum_pool(name="norms", bufs=1) as norms,
+        tc.psum_pool(name="dots", bufs=K) as dots,
+    ):
+        offsets = held.tile([P, K * COLS], U16, name="offsets")
+        nc.sync.dma_start(offsets[:], offs)
+
+        z_tiles = []
+        ctx_tiles = []
+        for h in range(CH):
+            z_h = held.tile([P, S], F32, name=f"z{h}")
+            nc.sync.dma_start(z_h[:], z[h * P : (h + 1) * P, :])
+            z_tiles.append(z_h)
+            ctx_h = held.tile([P, S], F32, name=f"ctx{h}")
+            nc.scalar.dma_start(ctx_h[:], ctx[h * P : (h + 1) * P, :])
+            ctx_tiles.append(ctx_h)
+
+        identity = held.tile([P, P], F32, name="identity")
+        make_identity(nc, identity[:])
+
+        inverse_norms = []
+        for name, tiles, scale in (("z", z_tiles, 1.0), ("ctx", ctx_tiles, TEMP * TEMP)):
+            square_sum = norms.tile([P, S], F32, name=f"{name}_square_sum")
+            for h in range(CH):
+                square = squares.tile([P, S], F32, name="square")
+                nc.scalar.activation(square[:], tiles[h][:], SQUARE)
+                nc.tensor.matmul(square_sum[:], identity[:], square[:], start=(h == 0), stop=(h == CH - 1))
+            inverse_norm = held.tile([P, S], F32, name=f"{name}_inverse_norm")
+            nc.scalar.activation(inverse_norm[:], square_sum[:], RSQRT, scale=scale)
+            inverse_norms.append(inverse_norm)
+        z_inverse_norm, ctx_inverse_norm = inverse_norms
+
+        def piece(k):
+            return offsets[:, k * COLS : (k + 1) * COLS]
+
+        def dot_products(k):
+            dot = dots.tile([P, S], F32, name="dot")
+            for h in range(CH):
+                product = products.tile([P, S], F32, name="product")
+                nc.vector.tensor_tensor(product[:], z_tiles[h][:].indirect(piece(k)), ctx_tiles[h][:], MULT)
+                nc.tensor.matmul(dot[:], identity[:], product[:], start=(h == 0), stop=(h == CH - 1))
+            return dot
+
+        def finish(k, dot):
+            weight = results.tile([P, S], F32, name="weight")
+            nc.vector.tensor_tensor(weight[:], z_inverse_norm[:].indirect(piece(k)), ctx_inverse_norm[:], MULT)
+            logits = results.tile([P, S], F32, name="logits")
+            nc.vector.tensor_tensor(logits[:], dot[:], weight[:], MULT)
+            nc.sync.dma_start(out[:, k * S : (k + 1) * S], logits[:])
+
+        earlier = None
+        for k in range(K):
+            dot = dot_products(k)
+            if earlier is not None:
+                finish(k - 1, earlier)
+            earlier = dot
+        finish(K - 1, earlier)

@@ -6,6 +6,7 @@ CH = 8
 S = 512
 K = 4
 TEMP = 0.5
+LAG = 2
 COLS = S // 16
 
 FLOPS = 2 * CH * P * K * S
@@ -13,6 +14,7 @@ FLOPS = 2 * CH * P * K * S
 F32 = mybir.dt.float32
 U16 = mybir.dt.uint16
 MULT = mybir.AluOpType.mult
+ADD = mybir.AluOpType.add
 SQUARE = mybir.ActivationFunctionType.Square
 RSQRT = mybir.ActivationFunctionType.Abs_reciprocal_sqrt
 
@@ -24,7 +26,6 @@ def tile_contrastivessl_kernel(tc, z, ctx, offs, out):
         tc.tile_pool(name="squares", bufs=4) as squares,
         tc.tile_pool(name="products", bufs=16) as products,
         tc.tile_pool(name="results", bufs=2) as results,
-        tc.psum_pool(name="norms", bufs=1) as norms,
         tc.psum_pool(name="dots", bufs=K) as dots,
     ):
         offsets = held.tile([P, K * COLS], U16, name="offsets")
@@ -45,11 +46,12 @@ def tile_contrastivessl_kernel(tc, z, ctx, offs, out):
 
         inverse_norms = []
         for name, tiles, scale in (("z", z_tiles, 1.0), ("ctx", ctx_tiles, TEMP * TEMP)):
-            square_sum = norms.tile([P, S], F32, name=f"{name}_square_sum")
-            for h in range(CH):
+            square_sum = held.tile([P, S], F32, name=f"{name}_square_sum")
+            nc.scalar.activation(square_sum[:], tiles[0][:], SQUARE)
+            for h in range(1, CH):
                 square = squares.tile([P, S], F32, name="square")
                 nc.scalar.activation(square[:], tiles[h][:], SQUARE)
-                nc.tensor.matmul(square_sum[:], identity[:], square[:], start=(h == 0), stop=(h == CH - 1))
+                nc.gpsimd.tensor_tensor(square_sum[:], square_sum[:], square[:], ADD)
             inverse_norm = held.tile([P, S], F32, name=f"{name}_inverse_norm")
             nc.scalar.activation(inverse_norm[:], square_sum[:], RSQRT, scale=scale)
             inverse_norms.append(inverse_norm)
@@ -73,10 +75,10 @@ def tile_contrastivessl_kernel(tc, z, ctx, offs, out):
             nc.vector.tensor_tensor(logits[:], dot[:], weight[:], MULT)
             nc.sync.dma_start(out[:, k * S : (k + 1) * S], logits[:])
 
-        earlier = None
+        dot_tiles = []
         for k in range(K):
-            dot = dot_products(k)
-            if earlier is not None:
-                finish(k - 1, earlier)
-            earlier = dot
-        finish(K - 1, earlier)
+            dot_tiles.append(dot_products(k))
+            if k >= LAG:
+                finish(k - LAG, dot_tiles[k - LAG])
+        for k in range(K - LAG, K):
+            finish(k, dot_tiles[k])

@@ -12,9 +12,9 @@ COLS = S // 16
 FLOPS = 2 * CH * P * K * S
 
 F32 = mybir.dt.float32
+BF16 = mybir.dt.bfloat16
 U16 = mybir.dt.uint16
 MULT = mybir.AluOpType.mult
-ADD = mybir.AluOpType.add
 SQUARE = mybir.ActivationFunctionType.Square
 RSQRT = mybir.ActivationFunctionType.Abs_reciprocal_sqrt
 
@@ -26,6 +26,7 @@ def tile_contrastivessl_kernel(tc, z, ctx, offs, out):
         tc.tile_pool(name="squares", bufs=4) as squares,
         tc.tile_pool(name="products", bufs=16) as products,
         tc.tile_pool(name="results", bufs=2) as results,
+        tc.psum_pool(name="norms", bufs=1) as norms,
         tc.psum_pool(name="dots", bufs=K) as dots,
     ):
         offsets = held.tile([P, K * COLS], U16, name="offsets")
@@ -44,14 +45,16 @@ def tile_contrastivessl_kernel(tc, z, ctx, offs, out):
         identity = held.tile([P, P], F32, name="identity")
         make_identity(nc, identity[:])
 
+        identity_bf16 = held.tile([P, P], BF16, name="identity_bf16")
+        make_identity(nc, identity_bf16[:])
+
         inverse_norms = []
         for name, tiles, scale in (("z", z_tiles, 1.0), ("ctx", ctx_tiles, TEMP * TEMP)):
-            square_sum = held.tile([P, S], F32, name=f"{name}_square_sum")
-            nc.scalar.activation(square_sum[:], tiles[0][:], SQUARE)
-            for h in range(1, CH):
-                square = squares.tile([P, S], F32, name="square")
+            square_sum = norms.tile([P, S], F32, name=f"{name}_square_sum")
+            for h in range(CH):
+                square = squares.tile([P, S], BF16, name="square")
                 nc.scalar.activation(square[:], tiles[h][:], SQUARE)
-                nc.gpsimd.tensor_tensor(square_sum[:], square_sum[:], square[:], ADD)
+                nc.tensor.matmul(square_sum[:], identity_bf16[:], square[:], start=(h == 0), stop=(h == CH - 1))
             inverse_norm = held.tile([P, S], F32, name=f"{name}_inverse_norm")
             nc.scalar.activation(inverse_norm[:], square_sum[:], RSQRT, scale=scale)
             inverse_norms.append(inverse_norm)

@@ -6,15 +6,15 @@ CH = 8
 S = 512
 K = 4
 TEMP = 0.5
-LAG = 2
+BLOCKS = S // P
 COLS = S // 16
 
 FLOPS = 2 * CH * P * K * S
 
 F32 = mybir.dt.float32
-BF16 = mybir.dt.bfloat16
 U16 = mybir.dt.uint16
 MULT = mybir.AluOpType.mult
+COPY = mybir.ActivationFunctionType.Copy
 SQUARE = mybir.ActivationFunctionType.Square
 RSQRT = mybir.ActivationFunctionType.Abs_reciprocal_sqrt
 
@@ -24,10 +24,10 @@ def tile_contrastivessl_kernel(tc, z, ctx, offs, out):
     with (
         tc.tile_pool(name="held", bufs=1) as held,
         tc.tile_pool(name="squares", bufs=4) as squares,
-        tc.tile_pool(name="products", bufs=16) as products,
+        tc.tile_pool(name="products", bufs=8) as products,
         tc.tile_pool(name="results", bufs=2) as results,
-        tc.psum_pool(name="norms", bufs=1) as norms,
-        tc.psum_pool(name="dots", bufs=K) as dots,
+        tc.psum_pool(name="sums", bufs=1) as sums,
+        tc.psum_pool(name="uprights", bufs=2) as uprights,
     ):
         offsets = held.tile([P, K * COLS], U16, name="offsets")
         nc.sync.dma_start(offsets[:], offs)
@@ -45,43 +45,53 @@ def tile_contrastivessl_kernel(tc, z, ctx, offs, out):
         identity = held.tile([P, P], F32, name="identity")
         make_identity(nc, identity[:])
 
-        identity_bf16 = held.tile([P, P], BF16, name="identity_bf16")
-        make_identity(nc, identity_bf16[:])
-
-        inverse_norms = []
-        for name, tiles, scale in (("z", z_tiles, 1.0), ("ctx", ctx_tiles, TEMP * TEMP)):
-            square_sum = norms.tile([P, S], F32, name=f"{name}_square_sum")
-            for h in range(CH):
-                square = squares.tile([P, S], BF16, name="square")
-                nc.scalar.activation(square[:], tiles[h][:], SQUARE)
-                nc.tensor.matmul(square_sum[:], identity_bf16[:], square[:], start=(h == 0), stop=(h == CH - 1))
-            inverse_norm = held.tile([P, S], F32, name=f"{name}_inverse_norm")
-            nc.scalar.activation(inverse_norm[:], square_sum[:], RSQRT, scale=scale)
-            inverse_norms.append(inverse_norm)
-        z_inverse_norm, ctx_inverse_norm = inverse_norms
+        def block(b):
+            return slice(b * P, (b + 1) * P)
 
         def piece(k):
             return offsets[:, k * COLS : (k + 1) * COLS]
 
-        def dot_products(k):
-            dot = dots.tile([P, S], F32, name="dot")
+        def add_flipped(flipped_sum, tile, h):
+            for b in range(BLOCKS):
+                nc.tensor.matmul(
+                    flipped_sum[:, block(b)],
+                    tile[:, block(b)],
+                    identity[:],
+                    is_transpose=True,
+                    start=(h == 0 and b == 0),
+                    stop=(h == CH - 1 and b == BLOCKS - 1),
+                )
+
+        def upright(flipped_sum, func, scale):
+            flipped = results.tile([P, S], F32, name="flipped")
+            nc.scalar.activation(flipped[:], flipped_sum[:], func, scale=scale)
+            bank = uprights.tile([P, S], F32, name="bank")
+            for b in range(BLOCKS):
+                nc.tensor.transpose(bank[:, block(b)], flipped[:, block(b)], identity[:])
+            return bank
+
+        inverse_norms = []
+        for name, tiles, scale in (("z", z_tiles, 1.0), ("ctx", ctx_tiles, TEMP * TEMP)):
+            square_sum = sums.tile([P, S], F32, name=f"{name}_square_sum")
             for h in range(CH):
+                square = squares.tile([P, S], F32, name="square")
+                nc.scalar.activation(square[:], tiles[h][:], SQUARE)
+                add_flipped(square_sum, square, h)
+            inverse_norm = held.tile([P, S], F32, name=f"{name}_inverse_norm")
+            nc.scalar.copy(inverse_norm[:], upright(square_sum, RSQRT, scale)[:])
+            inverse_norms.append(inverse_norm)
+        z_inverse_norm, ctx_inverse_norm = inverse_norms
+
+        dots = [sums.tile([P, S], F32, name=f"dot{k}") for k in range(K)]
+        for h in range(CH):
+            for k in range(K):
                 product = products.tile([P, S], F32, name="product")
                 nc.vector.tensor_tensor(product[:], z_tiles[h][:].indirect(piece(k)), ctx_tiles[h][:], MULT)
-                nc.tensor.matmul(dot[:], identity[:], product[:], start=(h == 0), stop=(h == CH - 1))
-            return dot
+                add_flipped(dots[k], product, h)
 
-        def finish(k, dot):
+        for k in range(K):
             weight = results.tile([P, S], F32, name="weight")
             nc.vector.tensor_tensor(weight[:], z_inverse_norm[:].indirect(piece(k)), ctx_inverse_norm[:], MULT)
             logits = results.tile([P, S], F32, name="logits")
-            nc.vector.tensor_tensor(logits[:], dot[:], weight[:], MULT)
+            nc.vector.tensor_tensor(logits[:], upright(dots[k], COPY, 1.0)[:], weight[:], MULT)
             nc.sync.dma_start(out[:, k * S : (k + 1) * S], logits[:])
-
-        dot_tiles = []
-        for k in range(K):
-            dot_tiles.append(dot_products(k))
-            if k >= LAG:
-                finish(k - LAG, dot_tiles[k - LAG])
-        for k in range(K - LAG, K):
-            finish(k, dot_tiles[k])

@@ -70,20 +70,19 @@ def tile_contrastivessl_kernel(tc, z, ctx, offs, out):
                 nc.tensor.transpose(bank[:, block(b)], flipped[:, block(b)], identity[:])
             return bank
 
-        inverse_norms = []
-        for name, tiles, scale in (("z", z_tiles, 1.0), ("ctx", ctx_tiles, TEMP * TEMP)):
-            square_sum = sums.tile([P, S], F32, name=f"{name}_square_sum")
-            for h in range(CH):
-                square = squares.tile([P, S], F32, name="square")
-                nc.scalar.activation(square[:], tiles[h][:], SQUARE)
-                add_flipped(square_sum, square, h)
-            inverse_norm = held.tile([P, S], F32, name=f"{name}_inverse_norm")
-            nc.scalar.copy(inverse_norm[:], upright(square_sum, RSQRT, scale)[:])
-            inverse_norms.append(inverse_norm)
-        z_inverse_norm, ctx_inverse_norm = inverse_norms
-
+        z_square_sum = sums.tile([P, S], F32, name="z_square_sum")
+        ctx_square_sum = sums.tile([P, S], F32, name="ctx_square_sum")
+        z_inverse_norm = held.tile([P, S], F32, name="z_inverse_norm")
+        ctx_inverse_norm = held.tile([P, S], F32, name="ctx_inverse_norm")
         dots = [sums.tile([P, S], F32, name=f"dot{k}") for k in range(K)]
         for h in range(CH):
+            for tile, square_sum in ((z_tiles[h], z_square_sum), (ctx_tiles[h], ctx_square_sum)):
+                square = squares.tile([P, S], F32, name="square")
+                nc.scalar.activation(square[:], tile[:], SQUARE)
+                add_flipped(square_sum, square, h)
+            if h == CH - 1:
+                nc.scalar.copy(z_inverse_norm[:], upright(z_square_sum, RSQRT, 1.0)[:])
+                nc.scalar.copy(ctx_inverse_norm[:], upright(ctx_square_sum, RSQRT, TEMP * TEMP)[:])
             for k in range(K):
                 product = products.tile([P, S], F32, name="product")
                 nc.vector.tensor_tensor(product[:], z_tiles[h][:].indirect(piece(k)), ctx_tiles[h][:], MULT)

@@ -24,10 +24,10 @@ def tile_contrastivessl_kernel(tc, z, ctx, offs, out):
     with (
         tc.tile_pool(name="held", bufs=1) as held,
         tc.tile_pool(name="squares", bufs=4) as squares,
-        tc.tile_pool(name="products", bufs=8) as products,
+        tc.tile_pool(name="products", bufs=16) as products,
         tc.tile_pool(name="results", bufs=2) as results,
-        tc.psum_pool(name="sums", bufs=1) as sums,
-        tc.psum_pool(name="uprights", bufs=2) as uprights,
+        tc.psum_pool(name="dot_banks", bufs=1) as dot_banks,
+        tc.psum_pool(name="spare_banks", bufs=4) as spare_banks,
     ):
         offsets = held.tile([P, K * COLS], U16, name="offsets")
         nc.sync.dma_start(offsets[:], offs)
@@ -39,7 +39,7 @@ def tile_contrastivessl_kernel(tc, z, ctx, offs, out):
             nc.sync.dma_start(z_h[:], z[h * P : (h + 1) * P, :])
             z_tiles.append(z_h)
             ctx_h = held.tile([P, S], F32, name=f"ctx{h}")
-            nc.scalar.dma_start(ctx_h[:], ctx[h * P : (h + 1) * P, :])
+            nc.sync.dma_start(ctx_h[:], ctx[h * P : (h + 1) * P, :])
             ctx_tiles.append(ctx_h)
 
         identity = held.tile([P, P], F32, name="identity")
@@ -65,22 +65,24 @@ def tile_contrastivessl_kernel(tc, z, ctx, offs, out):
         def upright(flipped_sum, func, scale):
             flipped = results.tile([P, S], F32, name="flipped")
             nc.scalar.activation(flipped[:], flipped_sum[:], func, scale=scale)
-            bank = uprights.tile([P, S], F32, name="bank")
+            bank = spare_banks.tile([P, S], F32, name="bank")
             for b in range(BLOCKS):
                 nc.tensor.transpose(bank[:, block(b)], flipped[:, block(b)], identity[:])
             return bank
 
-        z_square_sum = sums.tile([P, S], F32, name="z_square_sum")
-        ctx_square_sum = sums.tile([P, S], F32, name="ctx_square_sum")
+        z_square_sum = spare_banks.tile([P, S], F32, name="z_square_sum", tag="bank")
+        ctx_square_sum = spare_banks.tile([P, S], F32, name="ctx_square_sum", tag="bank")
         z_inverse_norm = held.tile([P, S], F32, name="z_inverse_norm")
         ctx_inverse_norm = held.tile([P, S], F32, name="ctx_inverse_norm")
-        dots = [sums.tile([P, S], F32, name=f"dot{k}") for k in range(K)]
+        dots = [dot_banks.tile([P, S], F32, name=f"dot{k}") for k in range(K)]
         for h in range(CH):
-            for tile, square_sum in ((z_tiles[h], z_square_sum), (ctx_tiles[h], ctx_square_sum)):
-                square = squares.tile([P, S], F32, name="square")
-                nc.scalar.activation(square[:], tile[:], SQUARE)
-                add_flipped(square_sum, square, h)
-            if h == CH - 1:
+            if h < CH // 2:
+                for c in (2 * h, 2 * h + 1):
+                    for tile, square_sum in ((z_tiles[c], z_square_sum), (ctx_tiles[c], ctx_square_sum)):
+                        square = squares.tile([P, S], F32, name="square")
+                        nc.scalar.activation(square[:], tile[:], SQUARE)
+                        add_flipped(square_sum, square, c)
+            if h == CH // 2:
                 nc.scalar.copy(z_inverse_norm[:], upright(z_square_sum, RSQRT, 1.0)[:])
                 nc.scalar.copy(ctx_inverse_norm[:], upright(ctx_square_sum, RSQRT, TEMP * TEMP)[:])
             for k in range(K):
@@ -88,9 +90,12 @@ def tile_contrastivessl_kernel(tc, z, ctx, offs, out):
                 nc.vector.tensor_tensor(product[:], z_tiles[h][:].indirect(piece(k)), ctx_tiles[h][:], MULT)
                 add_flipped(dots[k], product, h)
 
+        weights = []
         for k in range(K):
-            weight = results.tile([P, S], F32, name="weight")
+            weight = held.tile([P, S], F32, name=f"weight{k}")
             nc.vector.tensor_tensor(weight[:], z_inverse_norm[:].indirect(piece(k)), ctx_inverse_norm[:], MULT)
-            logits = results.tile([P, S], F32, name="logits")
-            nc.vector.tensor_tensor(logits[:], upright(dots[k], COPY, 1.0)[:], weight[:], MULT)
+            weights.append(weight)
+        for k in range(K):
+            logits = held.tile([P, S], F32, name=f"logits{k}")
+            nc.vector.tensor_tensor(logits[:], upright(dots[k], COPY, 1.0)[:], weights[k][:], MULT)
             nc.sync.dma_start(out[:, k * S : (k + 1) * S], logits[:])

@@ -24,7 +24,7 @@ def tile_contrastivessl_kernel(tc, z, ctx, offs, out):
     with (
         tc.tile_pool(name="held", bufs=1) as held,
         tc.tile_pool(name="squares", bufs=4) as squares,
-        tc.tile_pool(name="products", bufs=16) as products,
+        tc.tile_pool(name="products", bufs=32) as products,
         tc.tile_pool(name="results", bufs=2) as results,
         tc.psum_pool(name="dot_banks", bufs=1) as dot_banks,
         tc.psum_pool(name="spare_banks", bufs=4) as spare_banks,

@@ -5,7 +5,9 @@ P = 128
 CH = 8
 S = 512
 K = 4
+EARLY = 2
 TEMP = 0.5
+SHIFT = 2 / TEMP
 BLOCKS = S // P
 COLS = S // 16
 
@@ -17,6 +19,8 @@ MULT = mybir.AluOpType.mult
 COPY = mybir.ActivationFunctionType.Copy
 SQUARE = mybir.ActivationFunctionType.Square
 RSQRT = mybir.ActivationFunctionType.Abs_reciprocal_sqrt
+LN = mybir.ActivationFunctionType.Ln
+EXP = mybir.ActivationFunctionType.Exp
 
 
 def tile_contrastivessl_kernel(tc, z, ctx, offs, out):
@@ -24,10 +28,8 @@ def tile_contrastivessl_kernel(tc, z, ctx, offs, out):
     with (
         tc.tile_pool(name="held", bufs=1) as held,
         tc.tile_pool(name="squares", bufs=4) as squares,
-        tc.tile_pool(name="products", bufs=32) as products,
-        tc.tile_pool(name="results", bufs=2) as results,
-        tc.psum_pool(name="dot_banks", bufs=1) as dot_banks,
-        tc.psum_pool(name="spare_banks", bufs=4) as spare_banks,
+        tc.tile_pool(name="products", bufs=EARLY * CH) as products,
+        tc.tile_pool(name="flipped_tiles", bufs=4) as flipped_tiles,
     ):
         offsets = held.tile([P, K * COLS], U16, name="offsets")
         nc.sync.dma_start(offsets[:], offs)
@@ -51,51 +53,99 @@ def tile_contrastivessl_kernel(tc, z, ctx, offs, out):
         def piece(k):
             return offsets[:, k * COLS : (k + 1) * COLS]
 
-        def add_flipped(flipped_sum, tile, h):
+        def add_flipped(bank, tile, first, last):
             for b in range(BLOCKS):
                 nc.tensor.matmul(
-                    flipped_sum[:, block(b)],
+                    bank[:, block(b)],
                     tile[:, block(b)],
                     identity[:],
                     is_transpose=True,
-                    start=(h == 0 and b == 0),
-                    stop=(h == CH - 1 and b == BLOCKS - 1),
+                    start=(first and b == 0),
+                    stop=(last and b == BLOCKS - 1),
                 )
 
-        def upright(flipped_sum, func, scale):
-            flipped = results.tile([P, S], F32, name="flipped")
-            nc.scalar.activation(flipped[:], flipped_sum[:], func, scale=scale)
-            bank = spare_banks.tile([P, S], F32, name="bank")
-            for b in range(BLOCKS):
-                nc.tensor.transpose(bank[:, block(b)], flipped[:, block(b)], identity[:])
-            return bank
+        def look_up(k, h):
+            product = products.tile([P, S], F32, name="product")
+            nc.vector.tensor_tensor(product[:], z_tiles[h][:].indirect(piece(k)), ctx_tiles[h][:], MULT)
+            return product
 
-        z_square_sum = spare_banks.tile([P, S], F32, name="z_square_sum", tag="bank")
-        ctx_square_sum = spare_banks.tile([P, S], F32, name="ctx_square_sum", tag="bank")
-        z_inverse_norm = held.tile([P, S], F32, name="z_inverse_norm")
-        ctx_inverse_norm = held.tile([P, S], F32, name="ctx_inverse_norm")
-        dots = [dot_banks.tile([P, S], F32, name=f"dot{k}") for k in range(K)]
+        def weight(k):
+            weight_k = products.tile([P, S], F32, name="product")
+            nc.vector.tensor_tensor(weight_k[:], z_factor[:].indirect(piece(k)), ctx_factor[:], MULT)
+            return weight_k
+
+        early_products = [[None] * CH for k in range(EARLY)]
         for h in range(CH):
-            if h < CH // 2:
-                for c in (2 * h, 2 * h + 1):
-                    for tile, square_sum in ((z_tiles[c], z_square_sum), (ctx_tiles[c], ctx_square_sum)):
-                        square = squares.tile([P, S], F32, name="square")
-                        nc.scalar.activation(square[:], tile[:], SQUARE)
-                        add_flipped(square_sum, square, c)
-            if h == CH // 2:
-                nc.scalar.copy(z_inverse_norm[:], upright(z_square_sum, RSQRT, 1.0)[:])
-                nc.scalar.copy(ctx_inverse_norm[:], upright(ctx_square_sum, RSQRT, TEMP * TEMP)[:])
-            for k in range(K):
-                product = products.tile([P, S], F32, name="product")
-                nc.vector.tensor_tensor(product[:], z_tiles[h][:].indirect(piece(k)), ctx_tiles[h][:], MULT)
-                add_flipped(dots[k], product, h)
+            for k in range(EARLY):
+                early_products[k][h] = look_up(k, h)
 
-        weights = []
-        for k in range(K):
-            weight = held.tile([P, S], F32, name=f"weight{k}")
-            nc.vector.tensor_tensor(weight[:], z_inverse_norm[:].indirect(piece(k)), ctx_inverse_norm[:], MULT)
-            weights.append(weight)
-        for k in range(K):
-            logits = held.tile([P, S], F32, name=f"logits{k}")
-            nc.vector.tensor_tensor(logits[:], upright(dots[k], COPY, 1.0)[:], weights[k][:], MULT)
-            nc.sync.dma_start(out[:, k * S : (k + 1) * S], logits[:])
+        z_factor = held.tile([P, S], F32, name="z_factor")
+        ctx_factor = held.tile([P, S], F32, name="ctx_factor")
+        with tc.psum_pool(name="norm_banks", bufs=4) as norm_banks:
+            square_sums = [norm_banks.tile([P, S], F32, name=f"square_sum{i}", tag="bank") for i in range(2)]
+            for h in range(CH):
+                for tile, square_sum in ((z_tiles[h], square_sums[0]), (ctx_tiles[h], square_sums[1])):
+                    square = squares.tile([P, S], F32, name="square")
+                    nc.scalar.activation(square[:], tile[:], SQUARE)
+                    add_flipped(square_sum, square, h == 0, h == CH - 1)
+            for factor, square_sum, scale in (
+                (z_factor, square_sums[0], 1.0),
+                (ctx_factor, square_sums[1], TEMP * TEMP),
+            ):
+                flipped_factor = flipped_tiles.tile([P, S], F32, name="flipped")
+                nc.scalar.activation(flipped_factor[:], square_sum[:], RSQRT, scale=scale)
+                bank = norm_banks.tile([P, S], F32, name="bank")
+                add_flipped(bank, flipped_factor, True, True)
+                nc.scalar.copy(factor[:], bank[:])
+
+        with (
+            tc.psum_pool(name="dot_banks", bufs=1) as dot_banks,
+            tc.psum_pool(name="upright_banks", bufs=4) as upright_banks,
+        ):
+            dots = [dot_banks.tile([P, S], F32, name=f"dot{k}") for k in range(K)]
+
+            early = range(EARLY)
+            weights = [weight(k) for k in early]
+            logs = []
+            for k in early:
+                log = held.tile([P, S], F32, name=f"log{k}")
+                nc.scalar.activation(log[:], weights[k][:], LN, scale=1 / SHIFT)
+                logs.append(log)
+            for k in early:
+                for h in range(CH):
+                    add_flipped(dots[k], early_products[k][h], h == 0, False)
+            for k in early:
+                shift = held.tile([P, S], F32, name=f"shift{k}")
+                nc.scalar.activation(shift[:], logs[k][:], EXP, scale=-1.0)
+                add_flipped(dots[k], shift, False, True)
+            scaled_banks = []
+            for k in early:
+                flipped_log = flipped_tiles.tile([P, S], F32, name="flipped")
+                nc.scalar.activation(flipped_log[:], dots[k][:], LN)
+                bank = upright_banks.tile([P, S], F32, name="bank")
+                for b in range(BLOCKS):
+                    nc.tensor.matmul(
+                        bank[:, block(b)], flipped_log[:, block(b)], identity[:], is_transpose=True, start=(b == 0), stop=False
+                    )
+                nc.tensor.matmul(bank[:], identity[:], logs[k][:], start=False, stop=True)
+                scaled_banks.append(bank)
+            for k in early:
+                ratio = held.tile([P, S], F32, name=f"ratio{k}")
+                nc.scalar.activation(ratio[:], scaled_banks[k][:], EXP)
+                logits = held.tile([P, S], F32, name=f"logits{k}")
+                nc.scalar.activation(logits[:], ratio[:], COPY, scale=SHIFT, bias=-SHIFT)
+                nc.sync.dma_start(out[:, k * S : (k + 1) * S], logits[:])
+
+            for k in range(EARLY, K):
+                for h in range(CH):
+                    add_flipped(dots[k], look_up(k, h), h == 0, h == CH - 1)
+
+            late_weights = [weight(k) for k in range(EARLY, K)]
+            for k in range(EARLY, K):
+                flipped_dot = flipped_tiles.tile([P, S], F32, name="flipped")
+                nc.scalar.copy(flipped_dot[:], dots[k][:])
+                bank = upright_banks.tile([P, S], F32, name="bank")
+                add_flipped(bank, flipped_dot, True, True)
+                logits = held.tile([P, S], F32, name=f"logits{k}")
+                nc.vector.tensor_tensor(logits[:], bank[:], late_weights[k - EARLY][:], MULT)
+                nc.sync.dma_start(out[:, k * S : (k + 1) * S], logits[:])

@@ -6,6 +6,7 @@ CH = 8
 S = 512
 K = 4
 EARLY = 2
+AHEAD = 2
 TEMP = 0.5
 SHIFT = 2 / TEMP
 BLOCKS = S // P
@@ -27,7 +28,6 @@ def tile_contrastivessl_kernel(tc, z, ctx, offs, out):
     nc = tc.nc
     with (
         tc.tile_pool(name="held", bufs=1) as held,
-        tc.tile_pool(name="squares", bufs=4) as squares,
         tc.tile_pool(name="products", bufs=EARLY * CH) as products,
         tc.tile_pool(name="flipped_tiles", bufs=4) as flipped_tiles,
     ):
@@ -36,13 +36,12 @@ def tile_contrastivessl_kernel(tc, z, ctx, offs, out):
 
         z_tiles = []
         ctx_tiles = []
-        for h in range(CH):
-            z_h = held.tile([P, S], F32, name=f"z{h}")
-            nc.sync.dma_start(z_h[:], z[h * P : (h + 1) * P, :])
-            z_tiles.append(z_h)
-            ctx_h = held.tile([P, S], F32, name=f"ctx{h}")
-            nc.sync.dma_start(ctx_h[:], ctx[h * P : (h + 1) * P, :])
-            ctx_tiles.append(ctx_h)
+
+        def load(h):
+            for tiles, source, label in ((z_tiles, z, "z"), (ctx_tiles, ctx, "ctx")):
+                tile = held.tile([P, S], F32, name=f"{label}{h}")
+                nc.sync.dma_start(tile[:], source[h * P : (h + 1) * P, :])
+                tiles.append(tile)
 
         identity = held.tile([P, P], F32, name="identity")
         make_identity(nc, identity[:])
@@ -74,20 +73,25 @@ def tile_contrastivessl_kernel(tc, z, ctx, offs, out):
             nc.vector.tensor_tensor(weight_k[:], z_factor[:].indirect(piece(k)), ctx_factor[:], MULT)
             return weight_k
 
-        early_products = [[None] * CH for k in range(EARLY)]
-        for h in range(CH):
-            for k in range(EARLY):
-                early_products[k][h] = look_up(k, h)
-
         z_factor = held.tile([P, S], F32, name="z_factor")
         ctx_factor = held.tile([P, S], F32, name="ctx_factor")
         with tc.psum_pool(name="norm_banks", bufs=4) as norm_banks:
             square_sums = [norm_banks.tile([P, S], F32, name=f"square_sum{i}", tag="bank") for i in range(2)]
+            for h in range(AHEAD):
+                load(h)
             for h in range(CH):
-                for tile, square_sum in ((z_tiles[h], square_sums[0]), (ctx_tiles[h], square_sums[1])):
-                    square = squares.tile([P, S], F32, name="square")
+                for tile, square_sum, label in ((z_tiles[h], square_sums[0], "z"), (ctx_tiles[h], square_sums[1], "ctx")):
+                    square = held.tile([P, S], F32, name=f"{label}{h}_square", tag=f"{label}{h + AHEAD}")
                     nc.scalar.activation(square[:], tile[:], SQUARE)
                     add_flipped(square_sum, square, h == 0, h == CH - 1)
+                if h + AHEAD < CH:
+                    load(h + AHEAD)
+
+            early_products = [[None] * CH for k in range(EARLY)]
+            for h in range(CH):
+                for k in range(EARLY):
+                    early_products[k][h] = look_up(k, h)
+
             for factor, square_sum, scale in (
                 (z_factor, square_sums[0], 1.0),
                 (ctx_factor, square_sums[1], TEMP * TEMP),

@@ -6,7 +6,7 @@ CH = 8
 S = 512
 K = 4
 EARLY = 2
-AHEAD = 2
+AHEAD = 3
 TEMP = 0.5
 SHIFT = 2 / TEMP
 BLOCKS = S // P
@@ -68,8 +68,7 @@ def tile_contrastivessl_kernel(tc, z, ctx, offs, out):
             nc.vector.tensor_tensor(product[:], z_tiles[h][:].indirect(piece(k)), ctx_tiles[h][:], MULT)
             return product
 
-        def weight(k):
-            weight_k = products.tile([P, S], F32, name="product")
+        def weight(k, weight_k):
             nc.vector.tensor_tensor(weight_k[:], z_factor[:].indirect(piece(k)), ctx_factor[:], MULT)
             return weight_k
 
@@ -109,7 +108,7 @@ def tile_contrastivessl_kernel(tc, z, ctx, offs, out):
             dots = [dot_banks.tile([P, S], F32, name=f"dot{k}") for k in range(K)]
 
             early = range(EARLY)
-            weights = [weight(k) for k in early]
+            weights = [weight(k, held.tile([P, S], F32, name=f"weight{k}")) for k in early]
             logs = []
             for k in early:
                 log = held.tile([P, S], F32, name=f"log{k}")
@@ -144,7 +143,7 @@ def tile_contrastivessl_kernel(tc, z, ctx, offs, out):
                 for h in range(CH):
                     add_flipped(dots[k], look_up(k, h), h == 0, h == CH - 1)
 
-            late_weights = [weight(k) for k in range(EARLY, K)]
+            late_weights = [weight(k, products.tile([P, S], F32, name="product")) for k in range(EARLY, K)]
             for k in range(EARLY, K):
                 flipped_dot = flipped_tiles.tile([P, S], F32, name="flipped")
                 nc.scalar.copy(flipped_dot[:], dots[k][:])

@@ -150,5 +150,7 @@ def tile_contrastivessl_kernel(tc, z, ctx, offs, out):
                 bank = upright_banks.tile([P, S], F32, name="bank")
                 add_flipped(bank, flipped_dot, True, True)
                 logits = held.tile([P, S], F32, name=f"logits{k}")
-                nc.vector.tensor_tensor(logits[:], bank[:], late_weights[k - EARLY][:], MULT)
-                nc.sync.dma_start(out[:, k * S : (k + 1) * S], logits[:])
+                for start in (0, S // 2):
+                    part = slice(start, start + S // 2)
+                    nc.vector.tensor_tensor(logits[:, part], bank[:, part], late_weights[k - EARLY][:, part], MULT)
+                    nc.sync.dma_start(out[:, k * S + start : k * S + start + S // 2], logits[:, part])

import concourse.mybir as mybir
from concourse.masks import make_identity

P = 128
CH = 8
S = 512
K = 4
EARLY = 2
AHEAD = 3
TEMP = 0.5
SHIFT = 2 / TEMP
BLOCKS = S // P
COLS = S // 16

FLOPS = 2 * CH * P * K * S

F32 = mybir.dt.float32
U16 = mybir.dt.uint16
MULT = mybir.AluOpType.mult
COPY = mybir.ActivationFunctionType.Copy
SQUARE = mybir.ActivationFunctionType.Square
RSQRT = mybir.ActivationFunctionType.Abs_reciprocal_sqrt
LN = mybir.ActivationFunctionType.Ln
EXP = mybir.ActivationFunctionType.Exp


def tile_contrastivessl_kernel(tc, z, ctx, offs, out):
    nc = tc.nc
    with (
        tc.tile_pool(name="held", bufs=1) as held,
        tc.tile_pool(name="products", bufs=EARLY * CH) as products,
        tc.tile_pool(name="flipped_tiles", bufs=4) as flipped_tiles,
    ):
        offsets = held.tile([P, K * COLS], U16, name="offsets")
        nc.sync.dma_start(offsets[:], offs)

        z_tiles = []
        ctx_tiles = []

        def load(h):
            for tiles, source, label in ((z_tiles, z, "z"), (ctx_tiles, ctx, "ctx")):
                tile = held.tile([P, S], F32, name=f"{label}{h}")
                nc.sync.dma_start(tile[:], source[h * P : (h + 1) * P, :])
                tiles.append(tile)

        identity = held.tile([P, P], F32, name="identity")
        make_identity(nc, identity[:])

        def block(b):
            return slice(b * P, (b + 1) * P)

        def piece(k):
            return offsets[:, k * COLS : (k + 1) * COLS]

        def add_flipped(bank, tile, first, last):
            for b in range(BLOCKS):
                nc.tensor.matmul(
                    bank[:, block(b)],
                    tile[:, block(b)],
                    identity[:],
                    is_transpose=True,
                    start=(first and b == 0),
                    stop=(last and b == BLOCKS - 1),
                )

        def look_up(k, h):
            product = products.tile([P, S], F32, name="product")
            nc.vector.tensor_tensor(product[:], z_tiles[h][:].indirect(piece(k)), ctx_tiles[h][:], MULT)
            return product

        def weight(k, weight_k):
            nc.vector.tensor_tensor(weight_k[:], z_factor[:].indirect(piece(k)), ctx_factor[:], MULT)
            return weight_k

        z_factor = held.tile([P, S], F32, name="z_factor")
        ctx_factor = held.tile([P, S], F32, name="ctx_factor")
        with tc.psum_pool(name="norm_banks", bufs=4) as norm_banks:
            square_sums = [norm_banks.tile([P, S], F32, name=f"square_sum{i}", tag="bank") for i in range(2)]
            for h in range(AHEAD):
                load(h)
            for h in range(CH):
                for tile, square_sum, label in ((z_tiles[h], square_sums[0], "z"), (ctx_tiles[h], square_sums[1], "ctx")):
                    square = held.tile([P, S], F32, name=f"{label}{h}_square", tag=f"{label}{h + AHEAD}")
                    nc.scalar.activation(square[:], tile[:], SQUARE)
                    add_flipped(square_sum, square, h == 0, h == CH - 1)
                if h + AHEAD < CH:
                    load(h + AHEAD)

            early_products = [[None] * CH for k in range(EARLY)]
            for h in range(CH):
                for k in range(EARLY):
                    early_products[k][h] = look_up(k, h)

            for factor, square_sum, scale in (
                (z_factor, square_sums[0], 1.0),
                (ctx_factor, square_sums[1], TEMP * TEMP),
            ):
                flipped_factor = flipped_tiles.tile([P, S], F32, name="flipped")
                nc.scalar.activation(flipped_factor[:], square_sum[:], RSQRT, scale=scale)
                bank = norm_banks.tile([P, S], F32, name="bank")
                add_flipped(bank, flipped_factor, True, True)
                nc.scalar.copy(factor[:], bank[:])

        with (
            tc.psum_pool(name="dot_banks", bufs=1) as dot_banks,
            tc.psum_pool(name="upright_banks", bufs=4) as upright_banks,
        ):
            dots = [dot_banks.tile([P, S], F32, name=f"dot{k}") for k in range(K)]

            early = range(EARLY)
            weights = [weight(k, held.tile([P, S], F32, name=f"weight{k}")) for k in early]
            logs = []
            for k in early:
                log = held.tile([P, S], F32, name=f"log{k}")
                nc.scalar.activation(log[:], weights[k][:], LN, scale=1 / SHIFT)
                logs.append(log)
            for k in early:
                for h in range(CH):
                    add_flipped(dots[k], early_products[k][h], h == 0, False)
            for k in early:
                shift = held.tile([P, S], F32, name=f"shift{k}")
                nc.scalar.activation(shift[:], logs[k][:], EXP, scale=-1.0)
                add_flipped(dots[k], shift, False, True)
            scaled_banks = []
            for k in early:
                flipped_log = flipped_tiles.tile([P, S], F32, name="flipped")
                nc.scalar.activation(flipped_log[:], dots[k][:], LN)
                bank = upright_banks.tile([P, S], F32, name="bank")
                for b in range(BLOCKS):
                    nc.tensor.matmul(
                        bank[:, block(b)], flipped_log[:, block(b)], identity[:], is_transpose=True, start=(b == 0), stop=False
                    )
                nc.tensor.matmul(bank[:], identity[:], logs[k][:], start=False, stop=True)
                scaled_banks.append(bank)
            for k in early:
                ratio = held.tile([P, S], F32, name=f"ratio{k}")
                nc.scalar.activation(ratio[:], scaled_banks[k][:], EXP)
                logits = held.tile([P, S], F32, name=f"logits{k}")
                nc.scalar.activation(logits[:], ratio[:], COPY, scale=SHIFT, bias=-SHIFT)
                nc.sync.dma_start(out[:, k * S : (k + 1) * S], logits[:])

            for k in range(EARLY, K):
                for h in range(CH):
                    add_flipped(dots[k], look_up(k, h), h == 0, h == CH - 1)

            late_weights = [weight(k, products.tile([P, S], F32, name="product")) for k in range(EARLY, K)]
            for k in range(EARLY, K):
                flipped_dot = flipped_tiles.tile([P, S], F32, name="flipped")
                nc.scalar.copy(flipped_dot[:], dots[k][:])
                bank = upright_banks.tile([P, S], F32, name="bank")
                add_flipped(bank, flipped_dot, True, True)
                logits = held.tile([P, S], F32, name=f"logits{k}")
                for start in (0, S // 2):
                    part = slice(start, start + S // 2)
                    nc.vector.tensor_tensor(logits[:, part], bank[:, part], late_weights[k - EARLY][:, part], MULT)
                    nc.sync.dma_start(out[:, k * S + start : k * S + start + S // 2], logits[:, part])
